import numpy as np
import ml_dtypes

BF16 = ml_dtypes.bfloat16


def bf(x):
    return np.asarray(x, np.float32).astype(BF16)


def f32(x):
    return np.asarray(x, np.float32)


def f64(x):
    return np.asarray(x).astype(np.float64)


def striped(idx):
    return np.tile(idx.reshape(-1, 16).T, (8, 1))


B, C, S, K, H, N, E = 2, 256, 1024, 2, 512, 4096, 768


def setup_inputs():
    idx = np.concatenate([np.random.permutation(S)[:H] for _ in range(N // H)])
    return {"x": f32(np.random.standard_normal((B, C, S))), "w": bf(np.random.standard_normal((C, E)) / np.sqrt(C)), "bias": f32(0.1 * np.random.standard_normal((E, 1))), "offs": striped(idx)}


def reference(x, w, bias, offs):
    idx = offs[:16].T.reshape(-1)
    x, w, bias = f64(x), f64(w), f64(bias)
    P = N // B
    cols = []
    for b in range(B):
        piece = idx[b * P:(b + 1) * P]
        centre = np.tile(x[b], (1, K))
        d = (-x[b])[:, piece] + centre
        nf = centre - d
        q = w[:, :C].T @ nf
        k = w[:, C:C + C].T @ d
        v = w[:, C + C:].T @ nf
        cols.append(np.concatenate([q, k, v], axis=0))
    return np.concatenate(cols, axis=1) + bias

@@ -1,0 +1,75 @@
+import concourse.mybir as mybir
+
+F32, BF16, U16 = mybir.dt.float32, mybir.dt.bfloat16, mybir.dt.uint16
+ADD, SUBTRACT = mybir.AluOpType.add, mybir.AluOpType.subtract
+IDENTITY = mybir.ActivationFunctionType.Identity
+
+P = 128
+BATCHES, CHANNELS, NODES, SLOTS, FEATURES = 2, 256, 1024, 2, 768
+ENTRIES = BATCHES * SLOTS * NODES
+CHANNEL_BLOCKS = CHANNELS // P
+FEATURE_BLOCKS = FEATURES // P
+KEY_BLOCKS = (2, 3)
+CHUNK = 512
+CHUNKS = ENTRIES // CHUNK
+CHUNKS_PER_BATCH = CHUNKS // BATCHES
+OFFSET_COLUMNS = CHUNK // 16
+
+FLOPS = 2 * FEATURES * ENTRIES * CHANNELS
+
+
+def tile_graphtransformerblock_kernel(tc, x, w, bias, offs, out):
+    nc = tc.nc
+    with (
+        tc.tile_pool(name="held", bufs=1) as held,
+        tc.tile_pool(name="edges", bufs=2) as edges,
+        tc.tile_pool(name="staging", bufs=6) as staging,
+        tc.psum_pool(name="psum", bufs=8) as psum,
+    ):
+        offsets = held.tile([P, ENTRIES // 16], U16, name="offsets")
+        nc.sync.dma_start(offsets[:], offs)
+
+        centre = [[held.tile([P, NODES], F32, name=f"centre{b}{k}") for k in range(CHANNEL_BLOCKS)] for b in range(BATCHES)]
+        negated = [[held.tile([P, NODES], F32, name=f"negated{b}{k}") for k in range(CHANNEL_BLOCKS)] for b in range(BATCHES)]
+        weights = [held.tile([P, FEATURES], BF16, name=f"weights{k}") for k in range(CHANNEL_BLOCKS)]
+        for k in range(CHANNEL_BLOCKS):
+            nc.sync.dma_start(centre[0][k][:], x[0, k * P : (k + 1) * P, :])
+        for k in range(CHANNEL_BLOCKS):
+            nc.sync.dma_start(weights[k][:], w[k * P : (k + 1) * P, :])
+        for k in range(CHANNEL_BLOCKS):
+            nc.sync.dma_start(centre[1][k][:], x[1, k * P : (k + 1) * P, :])
+        bias_columns = held.tile([P, FEATURE_BLOCKS], F32, name="bias_columns")
+        with nc.allow_non_contiguous_dma(reason="768 single floats, once"):
+            nc.gpsimd.dma_start(bias_columns[:], bias.rearrange("(f p) one -> p (f one)", p=P))
+        for b in range(BATCHES):
+            for k in range(CHANNEL_BLOCKS):
+                nc.vector.tensor_scalar_mul(negated[b][k][:], centre[b][k][:], -1.0)
+
+        for r in range(CHUNKS):
+            b = r // CHUNKS_PER_BATCH
+            first_node = (r * CHUNK) % NODES
+            piece = offsets[:, r * OFFSET_COLUMNS : (r + 1) * OFFSET_COLUMNS]
+            d_bf16, nf_bf16 = [], []
+            for k in range(CHANNEL_BLOCKS):
+                here = centre[b][k][:, first_node : first_node + CHUNK]
+                d = edges.tile([P, CHUNK], F32, name=f"d{k}")
+                nc.vector.tensor_tensor(d[:], negated[b][k][:].indirect(piece), here, ADD)
+                d_bf16.append(edges.tile([P, CHUNK], BF16, name=f"d_bf16_{k}"))
+                nc.vector.tensor_copy(d_bf16[k][:], d[:])
+                nf_bf16.append(edges.tile([P, CHUNK], BF16, name=f"nf_bf16_{k}"))
+                nc.vector.tensor_tensor(nf_bf16[k][:], here, d[:], SUBTRACT)
+
+            for f in range(FEATURE_BLOCKS):
+                moving = d_bf16 if f in KEY_BLOCKS else nf_bf16
+                product = psum.tile([P, CHUNK], F32, name="product")
+                for k in range(CHANNEL_BLOCKS):
+                    nc.tensor.matmul(
+                        product[:],
+                        weights[k][:, f * P : (f + 1) * P],
+                        moving[k][:],
+                        start=(k == 0),
+                        stop=(k == CHANNEL_BLOCKS - 1),
+                    )
+                staged = staging.tile([P, CHUNK], F32, name="staged")
+                nc.scalar.activation(staged[:], product[:], IDENTITY, bias=bias_columns[:, f : f + 1])
+                nc.sync.dma_start(out[f * P : (f + 1) * P, r * CHUNK : (r + 1) * CHUNK], staged[:])

@@ -2,14 +2,15 @@ import concourse.mybir as mybir
 
 F32, BF16, U16 = mybir.dt.float32, mybir.dt.bfloat16, mybir.dt.uint16
 ADD, SUBTRACT = mybir.AluOpType.add, mybir.AluOpType.subtract
-IDENTITY = mybir.ActivationFunctionType.Identity
+IDENTITY, COPY = mybir.ActivationFunctionType.Identity, mybir.ActivationFunctionType.Copy
 
 P = 128
 BATCHES, CHANNELS, NODES, SLOTS, FEATURES = 2, 256, 1024, 2, 768
 ENTRIES = BATCHES * SLOTS * NODES
 CHANNEL_BLOCKS = CHANNELS // P
-FEATURE_BLOCKS = FEATURES // P
 KEY_BLOCKS = (2, 3)
+NEIGHBOUR_BLOCKS = (0, 1, 4, 5)
+FEATURE_BLOCKS = len(KEY_BLOCKS) + len(NEIGHBOUR_BLOCKS)
 CHUNK = 512
 CHUNKS = ENTRIES // CHUNK
 CHUNKS_PER_BATCH = CHUNKS // BATCHES
@@ -22,8 +23,8 @@ def tile_graphtransformerblock_kernel(tc, x, w, bias, offs, out):
     nc = tc.nc
     with (
         tc.tile_pool(name="held", bufs=1) as held,
-        tc.tile_pool(name="edges", bufs=2) as edges,
-        tc.tile_pool(name="staging", bufs=6) as staging,
+        tc.tile_pool(name="edges", bufs=3) as edges,
+        tc.tile_pool(name="staging", bufs=12) as staging,
         tc.psum_pool(name="psum", bufs=8) as psum,
     ):
         offsets = held.tile([P, ENTRIES // 16], U16, name="offsets")
@@ -32,44 +33,44 @@ def tile_graphtransformerblock_kernel(tc, x, w, bias, offs, out):
         centre = [[held.tile([P, NODES], F32, name=f"centre{b}{k}") for k in range(CHANNEL_BLOCKS)] for b in range(BATCHES)]
         negated = [[held.tile([P, NODES], F32, name=f"negated{b}{k}") for k in range(CHANNEL_BLOCKS)] for b in range(BATCHES)]
         weights = [held.tile([P, FEATURES], BF16, name=f"weights{k}") for k in range(CHANNEL_BLOCKS)]
-        for k in range(CHANNEL_BLOCKS):
-            nc.sync.dma_start(centre[0][k][:], x[0, k * P : (k + 1) * P, :])
-        for k in range(CHANNEL_BLOCKS):
-            nc.sync.dma_start(weights[k][:], w[k * P : (k + 1) * P, :])
-        for k in range(CHANNEL_BLOCKS):
-            nc.sync.dma_start(centre[1][k][:], x[1, k * P : (k + 1) * P, :])
         bias_columns = held.tile([P, FEATURE_BLOCKS], F32, name="bias_columns")
+        queues = (nc.scalar, nc.sync)
+        for k in range(CHANNEL_BLOCKS):
+            queues[k].dma_start(centre[0][k][:], x[0, k * P : (k + 1) * P, :])
+        for k in range(CHANNEL_BLOCKS):
+            queues[k].dma_start(weights[k][:], w[k * P : (k + 1) * P, :])
         with nc.allow_non_contiguous_dma(reason="768 single floats, once"):
-            nc.gpsimd.dma_start(bias_columns[:], bias.rearrange("(f p) one -> p (f one)", p=P))
-        for b in range(BATCHES):
-            for k in range(CHANNEL_BLOCKS):
-                nc.vector.tensor_scalar_mul(negated[b][k][:], centre[b][k][:], -1.0)
+            nc.sync.dma_start(bias_columns[:], bias.rearrange("(f p) one -> p (f one)", p=P))
+        for k in range(CHANNEL_BLOCKS):
+            queues[k].dma_start(centre[1][k][:], x[1, k * P : (k + 1) * P, :])
+
+        nc.vector.tensor_scalar_mul(negated[0][0][:], centre[0][0][:], -1.0)
+        for b, k in ((0, 1), (1, 0), (1, 1)):
+            nc.scalar.activation(negated[b][k][:], centre[b][k][:], COPY, scale=-1.0)
 
         for r in range(CHUNKS):
             b = r // CHUNKS_PER_BATCH
             first_node = (r * CHUNK) % NODES
             piece = offsets[:, r * OFFSET_COLUMNS : (r + 1) * OFFSET_COLUMNS]
-            d_bf16, nf_bf16 = [], []
+            product = {f: psum.tile([P, CHUNK], F32, name="product") for f in KEY_BLOCKS + NEIGHBOUR_BLOCKS}
             for k in range(CHANNEL_BLOCKS):
+                first, last = k == 0, k == CHANNEL_BLOCKS - 1
                 here = centre[b][k][:, first_node : first_node + CHUNK]
                 d = edges.tile([P, CHUNK], F32, name=f"d{k}")
                 nc.vector.tensor_tensor(d[:], negated[b][k][:].indirect(piece), here, ADD)
-                d_bf16.append(edges.tile([P, CHUNK], BF16, name=f"d_bf16_{k}"))
-                nc.vector.tensor_copy(d_bf16[k][:], d[:])
-                nf_bf16.append(edges.tile([P, CHUNK], BF16, name=f"nf_bf16_{k}"))
-                nc.vector.tensor_tensor(nf_bf16[k][:], here, d[:], SUBTRACT)
+                d_bf16 = edges.tile([P, CHUNK], BF16, name=f"d_bf16_{k}")
+                nc.vector.tensor_copy(d_bf16[:], d[:])
+                for f in KEY_BLOCKS:
+                    nc.tensor.matmul(product[f][:], weights[k][:, f * P : (f + 1) * P], d_bf16[:], start=first, stop=last)
+                nf_bf16 = edges.tile([P, CHUNK], BF16, name=f"nf_bf16_{k}")
+                nc.vector.tensor_tensor(nf_bf16[:], here, d[:], SUBTRACT)
+                for f in NEIGHBOUR_BLOCKS:
+                    nc.tensor.matmul(product[f][:], weights[k][:, f * P : (f + 1) * P], nf_bf16[:], start=first, stop=last)
 
-            for f in range(FEATURE_BLOCKS):
-                moving = d_bf16 if f in KEY_BLOCKS else nf_bf16
-                product = psum.tile([P, CHUNK], F32, name="product")
-                for k in range(CHANNEL_BLOCKS):
-                    nc.tensor.matmul(
-                        product[:],
-                        weights[k][:, f * P : (f + 1) * P],
-                        moving[k][:],
-                        start=(k == 0),
-                        stop=(k == CHANNEL_BLOCKS - 1),
-                    )
+            for turn, f in enumerate(KEY_BLOCKS + NEIGHBOUR_BLOCKS):
                 staged = staging.tile([P, CHUNK], F32, name="staged")
-                nc.scalar.activation(staged[:], product[:], IDENTITY, bias=bias_columns[:, f : f + 1])
+                if r == CHUNKS - 1 and turn % 2 == 1:
+                    nc.vector.tensor_scalar_add(staged[:], product[f][:], bias_columns[:, f : f + 1])
+                else:
+                    nc.scalar.activation(staged[:], product[f][:], IDENTITY, bias=bias_columns[:, f : f + 1])
                 nc.sync.dma_start(out[f * P : (f + 1) * P, r * CHUNK : (r + 1) * CHUNK], staged[:])

@@ -59,7 +59,7 @@ def tile_graphtransformerblock_kernel(tc, x, w, bias, offs, out):
                 d = edges.tile([P, CHUNK], F32, name=f"d{k}")
                 nc.vector.tensor_tensor(d[:], negated[b][k][:].indirect(piece), here, ADD)
                 d_bf16 = edges.tile([P, CHUNK], BF16, name=f"d_bf16_{k}")
-                nc.vector.tensor_copy(d_bf16[:], d[:])
+                nc.gpsimd.tensor_copy(d_bf16[:], d[:])
                 for f in KEY_BLOCKS:
                     nc.tensor.matmul(product[f][:], weights[k][:, f * P : (f + 1) * P], d_bf16[:], start=first, stop=last)
                 nf_bf16 = edges.tile([P, CHUNK], BF16, name=f"nf_bf16_{k}")

@@ -24,7 +24,7 @@ def tile_graphtransformerblock_kernel(tc, x, w, bias, offs, out):
     with (
         tc.tile_pool(name="held", bufs=1) as held,
         tc.tile_pool(name="edges", bufs=3) as edges,
-        tc.tile_pool(name="staging", bufs=12) as staging,
+        tc.tile_pool(name="staging", bufs=6) as staging,
         tc.psum_pool(name="psum", bufs=8) as psum,
     ):
         offsets = held.tile([P, ENTRIES // 16], U16, name="offsets")
@@ -59,7 +59,7 @@ def tile_graphtransformerblock_kernel(tc, x, w, bias, offs, out):
                 d = edges.tile([P, CHUNK], F32, name=f"d{k}")
                 nc.vector.tensor_tensor(d[:], negated[b][k][:].indirect(piece), here, ADD)
                 d_bf16 = edges.tile([P, CHUNK], BF16, name=f"d_bf16_{k}")
-                nc.gpsimd.tensor_copy(d_bf16[:], d[:])
+                nc.vector.tensor_copy(d_bf16[:], d[:])
                 for f in KEY_BLOCKS:
                     nc.tensor.matmul(product[f][:], weights[k][:, f * P : (f + 1) * P], d_bf16[:], start=first, stop=last)
                 nf_bf16 = edges.tile([P, CHUNK], BF16, name=f"nf_bf16_{k}")
@@ -67,10 +67,13 @@ def tile_graphtransformerblock_kernel(tc, x, w, bias, offs, out):
                 for f in NEIGHBOUR_BLOCKS:
                     nc.tensor.matmul(product[f][:], weights[k][:, f * P : (f + 1) * P], nf_bf16[:], start=first, stop=last)
 
-            for turn, f in enumerate(KEY_BLOCKS + NEIGHBOUR_BLOCKS):
-                staged = staging.tile([P, CHUNK], F32, name="staged")
-                if r == CHUNKS - 1 and turn % 2 == 1:
-                    nc.vector.tensor_scalar_add(staged[:], product[f][:], bias_columns[:, f : f + 1])
-                else:
-                    nc.scalar.activation(staged[:], product[f][:], IDENTITY, bias=bias_columns[:, f : f + 1])
-                nc.sync.dma_start(out[f * P : (f + 1) * P, r * CHUNK : (r + 1) * CHUNK], staged[:])
+            for first_block in (KEY_BLOCKS[0], NEIGHBOUR_BLOCKS[0], NEIGHBOUR_BLOCKS[2]):
+                staged = staging.tile([P, 2, CHUNK], F32, name="staged")
+                for half in range(2):
+                    f = first_block + half
+                    if r == CHUNKS - 1 and half == 1:
+                        nc.vector.tensor_scalar_add(staged[:, half, :], product[f][:], bias_columns[:, f : f + 1])
+                    else:
+                        nc.scalar.activation(staged[:, half, :], product[f][:], IDENTITY, bias=bias_columns[:, f : f + 1])
+                rows = out[first_block * P : (first_block + 2) * P, r * CHUNK : (r + 1) * CHUNK]
+                nc.sync.dma_start(rows.rearrange("(half p) n -> p half n", p=P), staged[:])

@@ -24,7 +24,7 @@ def tile_graphtransformerblock_kernel(tc, x, w, bias, offs, out):
     with (
         tc.tile_pool(name="held", bufs=1) as held,
         tc.tile_pool(name="edges", bufs=3) as edges,
-        tc.tile_pool(name="staging", bufs=6) as staging,
+        tc.tile_pool(name="staging", bufs=12) as staging,
         tc.psum_pool(name="psum", bufs=8) as psum,
     ):
         offsets = held.tile([P, ENTRIES // 16], U16, name="offsets")
@@ -53,27 +53,25 @@ def tile_graphtransformerblock_kernel(tc, x, w, bias, offs, out):
             first_node = (r * CHUNK) % NODES
             piece = offsets[:, r * OFFSET_COLUMNS : (r + 1) * OFFSET_COLUMNS]
             product = {f: psum.tile([P, CHUNK], F32, name="product") for f in KEY_BLOCKS + NEIGHBOUR_BLOCKS}
+            here = [centre[b][k][:, first_node : first_node + CHUNK] for k in range(CHANNEL_BLOCKS)]
+            d = [edges.tile([P, CHUNK], F32, name=f"d{k}") for k in range(CHANNEL_BLOCKS)]
+            for k in range(CHANNEL_BLOCKS):
+                nc.vector.tensor_tensor(d[k][:], negated[b][k][:].indirect(piece), here[k], ADD)
             for k in range(CHANNEL_BLOCKS):
                 first, last = k == 0, k == CHANNEL_BLOCKS - 1
-                here = centre[b][k][:, first_node : first_node + CHUNK]
-                d = edges.tile([P, CHUNK], F32, name=f"d{k}")
-                nc.vector.tensor_tensor(d[:], negated[b][k][:].indirect(piece), here, ADD)
                 d_bf16 = edges.tile([P, CHUNK], BF16, name=f"d_bf16_{k}")
-                nc.vector.tensor_copy(d_bf16[:], d[:])
+                nc.vector.tensor_copy(d_bf16[:], d[k][:])
                 for f in KEY_BLOCKS:
                     nc.tensor.matmul(product[f][:], weights[k][:, f * P : (f + 1) * P], d_bf16[:], start=first, stop=last)
                 nf_bf16 = edges.tile([P, CHUNK], BF16, name=f"nf_bf16_{k}")
-                nc.vector.tensor_tensor(nf_bf16[:], here, d[:], SUBTRACT)
+                nc.vector.tensor_tensor(nf_bf16[:], here[k], d[k][:], SUBTRACT)
                 for f in NEIGHBOUR_BLOCKS:
                     nc.tensor.matmul(product[f][:], weights[k][:, f * P : (f + 1) * P], nf_bf16[:], start=first, stop=last)
 
-            for first_block in (KEY_BLOCKS[0], NEIGHBOUR_BLOCKS[0], NEIGHBOUR_BLOCKS[2]):
-                staged = staging.tile([P, 2, CHUNK], F32, name="staged")
-                for half in range(2):
-                    f = first_block + half
-                    if r == CHUNKS - 1 and half == 1:
-                        nc.vector.tensor_scalar_add(staged[:, half, :], product[f][:], bias_columns[:, f : f + 1])
-                    else:
-                        nc.scalar.activation(staged[:, half, :], product[f][:], IDENTITY, bias=bias_columns[:, f : f + 1])
-                rows = out[first_block * P : (first_block + 2) * P, r * CHUNK : (r + 1) * CHUNK]
-                nc.sync.dma_start(rows.rearrange("(half p) n -> p half n", p=P), staged[:])
+            for turn, f in enumerate(KEY_BLOCKS + NEIGHBOUR_BLOCKS):
+                staged = staging.tile([P, CHUNK], F32, name="staged")
+                if r == CHUNKS - 1 and turn % 2 == 1:
+                    nc.vector.tensor_scalar_add(staged[:], product[f][:], bias_columns[:, f : f + 1])
+                else:
+                    nc.scalar.activation(staged[:], product[f][:], IDENTITY, bias=bias_columns[:, f : f + 1])
+                nc.sync.dma_start(out[f * P : (f + 1) * P, r * CHUNK : (r + 1) * CHUNK], staged[:])

@@ -58,15 +58,15 @@ def tile_graphtransformerblock_kernel(tc, x, w, bias, offs, out):
             for k in range(CHANNEL_BLOCKS):
                 nc.vector.tensor_tensor(d[k][:], negated[b][k][:].indirect(piece), here[k], ADD)
             for k in range(CHANNEL_BLOCKS):
-                first, last = k == 0, k == CHANNEL_BLOCKS - 1
                 d_bf16 = edges.tile([P, CHUNK], BF16, name=f"d_bf16_{k}")
                 nc.vector.tensor_copy(d_bf16[:], d[k][:])
                 for f in KEY_BLOCKS:
-                    nc.tensor.matmul(product[f][:], weights[k][:, f * P : (f + 1) * P], d_bf16[:], start=first, stop=last)
+                    nc.tensor.matmul(product[f][:], weights[k][:, f * P : (f + 1) * P], d_bf16[:], start=k == 0, stop=k == CHANNEL_BLOCKS - 1)
+            for k in range(CHANNEL_BLOCKS):
                 nf_bf16 = edges.tile([P, CHUNK], BF16, name=f"nf_bf16_{k}")
                 nc.vector.tensor_tensor(nf_bf16[:], here[k], d[k][:], SUBTRACT)
                 for f in NEIGHBOUR_BLOCKS:
-                    nc.tensor.matmul(product[f][:], weights[k][:, f * P : (f + 1) * P], nf_bf16[:], start=first, stop=last)
+                    nc.tensor.matmul(product[f][:], weights[k][:, f * P : (f + 1) * P], nf_bf16[:], start=k == 0, stop=k == CHANNEL_BLOCKS - 1)
 
             for turn, f in enumerate(KEY_BLOCKS + NEIGHBOUR_BLOCKS):
                 staged = staging.tile([P, CHUNK], F32, name="staged")

@@ -44,9 +44,10 @@ def tile_graphtransformerblock_kernel(tc, x, w, bias, offs, out):
         for k in range(CHANNEL_BLOCKS):
             queues[k].dma_start(centre[1][k][:], x[1, k * P : (k + 1) * P, :])
 
-        nc.vector.tensor_scalar_mul(negated[0][0][:], centre[0][0][:], -1.0)
-        for b, k in ((0, 1), (1, 0), (1, 1)):
-            nc.scalar.activation(negated[b][k][:], centre[b][k][:], COPY, scale=-1.0)
+        for k in range(CHANNEL_BLOCKS):
+            nc.vector.tensor_scalar_mul(negated[0][k][:], centre[0][k][:], -1.0)
+        for k in range(CHANNEL_BLOCKS):
+            nc.scalar.activation(negated[1][k][:], centre[1][k][:], COPY, scale=-1.0)
 
         for r in range(CHUNKS):
             b = r // CHUNKS_PER_BATCH

@@ -28,24 +28,24 @@ def tile_graphtransformerblock_kernel(tc, x, w, bias, offs, out):
         tc.psum_pool(name="psum", bufs=8) as psum,
     ):
         offsets = held.tile([P, ENTRIES // 16], U16, name="offsets")
-        nc.sync.dma_start(offsets[:], offs)
 
         centre = [[held.tile([P, NODES], F32, name=f"centre{b}{k}") for k in range(CHANNEL_BLOCKS)] for b in range(BATCHES)]
         negated = [[held.tile([P, NODES], F32, name=f"negated{b}{k}") for k in range(CHANNEL_BLOCKS)] for b in range(BATCHES)]
-        weights = [held.tile([P, FEATURES], BF16, name=f"weights{k}") for k in range(CHANNEL_BLOCKS)]
+        weights = held.tile([P, CHANNEL_BLOCKS, FEATURES], BF16, name="weights")
         bias_columns = held.tile([P, FEATURE_BLOCKS], F32, name="bias_columns")
+        with nc.allow_non_contiguous_dma(reason="768 single floats, once"):
+            nc.gpsimd.dma_start(bias_columns[:], bias.rearrange("(f p) one -> p (f one)", p=P))
         queues = (nc.scalar, nc.sync)
         for k in range(CHANNEL_BLOCKS):
-            queues[k].dma_start(centre[0][k][:], x[0, k * P : (k + 1) * P, :])
-        for k in range(CHANNEL_BLOCKS):
-            queues[k].dma_start(weights[k][:], w[k * P : (k + 1) * P, :])
-        with nc.allow_non_contiguous_dma(reason="768 single floats, once"):
-            nc.sync.dma_start(bias_columns[:], bias.rearrange("(f p) one -> p (f one)", p=P))
+            for h, queue in enumerate(queues):
+                half = slice(h * NODES // 2, (h + 1) * NODES // 2)
+                queue.dma_start(centre[0][k][:, half], x[0, k * P : (k + 1) * P, half])
+            if k == 0:
+                nc.sync.dma_start(offsets[:], offs)
+        nc.scalar.dma_start(weights[:], w.rearrange("(k p) n -> p k n", p=P))
         for k in range(CHANNEL_BLOCKS):
             queues[k].dma_start(centre[1][k][:], x[1, k * P : (k + 1) * P, :])
 
-        for k in range(CHANNEL_BLOCKS):
-            nc.vector.tensor_scalar_mul(negated[0][k][:], centre[0][k][:], -1.0)
         for k in range(CHANNEL_BLOCKS):
             nc.scalar.activation(negated[1][k][:], centre[1][k][:], COPY, scale=-1.0)
 
@@ -57,17 +57,21 @@ def tile_graphtransformerblock_kernel(tc, x, w, bias, offs, out):
             here = [centre[b][k][:, first_node : first_node + CHUNK] for k in range(CHANNEL_BLOCKS)]
             d = [edges.tile([P, CHUNK], F32, name=f"d{k}") for k in range(CHANNEL_BLOCKS)]
             for k in range(CHANNEL_BLOCKS):
+                if r == 0:
+                    for h in range(2):
+                        half = slice(h * NODES // 2, (h + 1) * NODES // 2)
+                        nc.vector.tensor_scalar_mul(negated[b][k][:, half], centre[b][k][:, half], -1.0)
                 nc.vector.tensor_tensor(d[k][:], negated[b][k][:].indirect(piece), here[k], ADD)
             for k in range(CHANNEL_BLOCKS):
                 d_bf16 = edges.tile([P, CHUNK], BF16, name=f"d_bf16_{k}")
                 nc.vector.tensor_copy(d_bf16[:], d[k][:])
                 for f in KEY_BLOCKS:
-                    nc.tensor.matmul(product[f][:], weights[k][:, f * P : (f + 1) * P], d_bf16[:], start=k == 0, stop=k == CHANNEL_BLOCKS - 1)
+                    nc.tensor.matmul(product[f][:], weights[:, k, f * P : (f + 1) * P], d_bf16[:], start=k == 0, stop=k == CHANNEL_BLOCKS - 1)
             for k in range(CHANNEL_BLOCKS):
                 nf_bf16 = edges.tile([P, CHUNK], BF16, name=f"nf_bf16_{k}")
                 nc.vector.tensor_tensor(nf_bf16[:], here[k], d[k][:], SUBTRACT)
                 for f in NEIGHBOUR_BLOCKS:
-                    nc.tensor.matmul(product[f][:], weights[k][:, f * P : (f + 1) * P], nf_bf16[:], start=k == 0, stop=k == CHANNEL_BLOCKS - 1)
+                    nc.tensor.matmul(product[f][:], weights[:, k, f * P : (f + 1) * P], nf_bf16[:], start=k == 0, stop=k == CHANNEL_BLOCKS - 1)
 
             for turn, f in enumerate(KEY_BLOCKS + NEIGHBOUR_BLOCKS):
                 staged = staging.tile([P, CHUNK], F32, name="staged")

import concourse.mybir as mybir

F32, BF16, U16 = mybir.dt.float32, mybir.dt.bfloat16, mybir.dt.uint16
ADD, SUBTRACT = mybir.AluOpType.add, mybir.AluOpType.subtract
IDENTITY, COPY = mybir.ActivationFunctionType.Identity, mybir.ActivationFunctionType.Copy

P = 128
BATCHES, CHANNELS, NODES, SLOTS, FEATURES = 2, 256, 1024, 2, 768
ENTRIES = BATCHES * SLOTS * NODES
CHANNEL_BLOCKS = CHANNELS // P
KEY_BLOCKS = (2, 3)
NEIGHBOUR_BLOCKS = (0, 1, 4, 5)
FEATURE_BLOCKS = len(KEY_BLOCKS) + len(NEIGHBOUR_BLOCKS)
CHUNK = 512
CHUNKS = ENTRIES // CHUNK
CHUNKS_PER_BATCH = CHUNKS // BATCHES
OFFSET_COLUMNS = CHUNK // 16

FLOPS = 2 * FEATURES * ENTRIES * CHANNELS


def tile_graphtransformerblock_kernel(tc, x, w, bias, offs, out):
    nc = tc.nc
    with (
        tc.tile_pool(name="held", bufs=1) as held,
        tc.tile_pool(name="edges", bufs=3) as edges,
        tc.tile_pool(name="staging", bufs=12) as staging,
        tc.psum_pool(name="psum", bufs=8) as psum,
    ):
        offsets = held.tile([P, ENTRIES // 16], U16, name="offsets")

        centre = [[held.tile([P, NODES], F32, name=f"centre{b}{k}") for k in range(CHANNEL_BLOCKS)] for b in range(BATCHES)]
        negated = [[held.tile([P, NODES], F32, name=f"negated{b}{k}") for k in range(CHANNEL_BLOCKS)] for b in range(BATCHES)]
        weights = held.tile([P, CHANNEL_BLOCKS, FEATURES], BF16, name="weights")
        bias_columns = held.tile([P, FEATURE_BLOCKS], F32, name="bias_columns")
        with nc.allow_non_contiguous_dma(reason="768 single floats, once"):
            nc.gpsimd.dma_start(bias_columns[:], bias.rearrange("(f p) one -> p (f one)", p=P))
        queues = (nc.scalar, nc.sync)
        for k in range(CHANNEL_BLOCKS):
            for h, queue in enumerate(queues):
                half = slice(h * NODES // 2, (h + 1) * NODES // 2)
                queue.dma_start(centre[0][k][:, half], x[0, k * P : (k + 1) * P, half])
            if k == 0:
                nc.sync.dma_start(offsets[:], offs)
        nc.scalar.dma_start(weights[:], w.rearrange("(k p) n -> p k n", p=P))
        for k in range(CHANNEL_BLOCKS):
            queues[k].dma_start(centre[1][k][:], x[1, k * P : (k + 1) * P, :])

        for k in range(CHANNEL_BLOCKS):
            nc.scalar.activation(negated[1][k][:], centre[1][k][:], COPY, scale=-1.0)

        for r in range(CHUNKS):
            b = r // CHUNKS_PER_BATCH
            first_node = (r * CHUNK) % NODES
            piece = offsets[:, r * OFFSET_COLUMNS : (r + 1) * OFFSET_COLUMNS]
            product = {f: psum.tile([P, CHUNK], F32, name="product") for f in KEY_BLOCKS + NEIGHBOUR_BLOCKS}
            here = [centre[b][k][:, first_node : first_node + CHUNK] for k in range(CHANNEL_BLOCKS)]
            d = [edges.tile([P, CHUNK], F32, name=f"d{k}") for k in range(CHANNEL_BLOCKS)]
            for k in range(CHANNEL_BLOCKS):
                if r == 0:
                    for h in range(2):
                        half = slice(h * NODES // 2, (h + 1) * NODES // 2)
                        nc.vector.tensor_scalar_mul(negated[b][k][:, half], centre[b][k][:, half], -1.0)
                nc.vector.tensor_tensor(d[k][:], negated[b][k][:].indirect(piece), here[k], ADD)
            for k in range(CHANNEL_BLOCKS):
                d_bf16 = edges.tile([P, CHUNK], BF16, name=f"d_bf16_{k}")
                nc.vector.tensor_copy(d_bf16[:], d[k][:])
                for f in KEY_BLOCKS:
                    nc.tensor.matmul(product[f][:], weights[:, k, f * P : (f + 1) * P], d_bf16[:], start=k == 0, stop=k == CHANNEL_BLOCKS - 1)
            for k in range(CHANNEL_BLOCKS):
                nf_bf16 = edges.tile([P, CHUNK], BF16, name=f"nf_bf16_{k}")
                nc.vector.tensor_tensor(nf_bf16[:], here[k], d[k][:], SUBTRACT)
                for f in NEIGHBOUR_BLOCKS:
                    nc.tensor.matmul(product[f][:], weights[:, k, f * P : (f + 1) * P], nf_bf16[:], start=k == 0, stop=k == CHANNEL_BLOCKS - 1)

            for turn, f in enumerate(KEY_BLOCKS + NEIGHBOUR_BLOCKS):
                staged = staging.tile([P, CHUNK], F32, name="staged")
                if r == CHUNKS - 1 and turn % 2 == 1:
                    nc.vector.tensor_scalar_add(staged[:], product[f][:], bias_columns[:, f : f + 1])
                else:
                    nc.scalar.activation(staged[:], product[f][:], IDENTITY, bias=bias_columns[:, f : f + 1])
                nc.sync.dma_start(out[f * P : (f + 1) * P, r * CHUNK : (r + 1) * CHUNK], staged[:])
